import numpy as np
import ml_dtypes


def mxq(x, axis, fmt="e4m3"):
    dtype, down = {"e4m3": (ml_dtypes.float8_e4m3fn, 7), "e5m2": (ml_dtypes.float8_e5m2, 14)}[fmt]
    v = np.moveaxis(np.asarray(x, np.float32).astype(ml_dtypes.bfloat16).astype(np.float64), axis, -1)
    blocks = v.reshape(v.shape[:-1] + (-1, 32))
    amax = np.abs(blocks).max(-1, keepdims=True)
    byte = np.maximum(np.where(amax > 0, np.frexp(amax)[1] - 1 + 127, 0) - down, 1)
    scale = np.exp2(byte - 127.0)
    codes = (blocks / scale).astype(np.float32).astype(dtype).astype(np.float64)
    return np.moveaxis((codes * scale).reshape(v.shape), -1, axis)


WIDE = False


def mx_kscale(k):
    if not WIDE:
        return np.ones(k)
    levels = np.array([10, -10, 5, -5, 0])
    if k % 512:
        return np.exp2(np.random.permutation(np.resize(levels, k // 32))).repeat(32)
    a = np.empty((k // 512, 16))
    for p in range(k // 512):
        a[p, :8] = np.random.permutation(np.resize(levels, 8))
        for g in range(8):
            far = levels[np.abs(levels - a[p, g]) >= 10]
            a[p, g + 8] = far[np.random.randint(len(far))]
    return np.exp2(a.ravel()).repeat(32)


BF16 = ml_dtypes.bfloat16


def bf(x):
    return np.asarray(x, np.float32).astype(BF16)


def f64(x):
    return np.asarray(x).astype(np.float64)


B, S, IN, OUT = 4, 2048, 1024, 256


def setup_inputs():
    s = mx_kscale(IN)
    w = np.random.standard_normal((OUT, IN + 1))
    w[:, :IN] *= 0.25 / np.sqrt(IN) / s
    w[:, IN] *= 0.5
    return {"x": bf(np.random.standard_normal((B, S, IN)) * s), "weight": bf(w)}


def reference(x, weight):
    w = f64(weight)
    in_features = w.shape[1] - 1
    xf = f64(x).reshape(-1, in_features)
    wm, wb = w[:, :in_features], w[:, in_features]
    xq = mxq(xf, 1, "e4m3")
    wq = mxq(wm, 1, "e4m3")
    lin = (xq @ wq.T) + wb
    ab = (np.abs(xq) @ np.abs(wq).T) + np.abs(wb)
    return 0.5 * (lin + ab)

@@ -1,0 +1,243 @@
+from contextlib import ExitStack
+
+import concourse.mybir as mybir
+from concourse.masks import make_identity
+
+F32 = mybir.dt.float32
+BF16 = mybir.dt.bfloat16
+I32 = mybir.dt.int32
+U32 = mybir.dt.uint32
+U8 = mybir.dt.uint8
+FP8X4 = mybir.dt.float8_e4m3fn_x4
+ALU = mybir.AluOpType
+ACT = mybir.ActivationFunctionType
+
+P = 128
+TOKENS = 8192
+IN = 1024
+OUT = 256
+PACK = 4
+PASSES = IN // (P * PACK)
+HALVES = 2
+ROW_WORDS = IN // 2
+BLOCKS = ROW_WORDS // P
+OUT_TILES = OUT // P
+
+TILES = 4
+CHUNK = TILES * P
+CHUNKS = TOKENS // CHUNK
+PAIR = 2
+BANKS = TILES // PAIR
+LAG = 2
+VECTOR_ABS_TILES = 2
+
+SIGNLESS = 0x7FFF7FFF
+
+FLOPS = 2 * 2 * TOKENS * IN * OUT
+
+
+def tile_skanlinear_t_kernel(tc, x, weight, out):
+    nc = tc.nc
+    x_rows = x.flatten_outer_dims()
+
+    with ExitStack() as stack:
+        const = stack.enter_context(tc.tile_pool(name="const", bufs=1))
+        x_pool = stack.enter_context(tc.tile_pool(name="x", bufs=CHUNKS))
+        grouped_pool = stack.enter_context(tc.tile_pool(name="grouped", bufs=2))
+        codes_pool = stack.enter_context(tc.tile_pool(name="codes", bufs=LAG + 1))
+        y_pool = stack.enter_context(tc.tile_pool(name="y", bufs=3 * BANKS))
+        xt_pool = stack.enter_context(tc.psum_pool(name="xt", bufs=4))
+        acc_pool = stack.enter_context(tc.psum_pool(name="acc", bufs=4))
+        stack.enter_context(tc.manual_schedule())
+
+        ident_f32 = const.tile([P, P], F32)
+        make_identity(nc, ident_f32[:])
+        ident_bf16 = const.tile([P, P], BF16)
+        make_identity(nc, ident_bf16[:])
+
+        def load_chunk(c, pieces):
+            x_sb = x_pool.tile([P, TILES * IN], BF16, name="x_sb")
+            rows = x_rows[c * CHUNK : (c + 1) * CHUNK, :].rearrange("(p j) k -> p (j k)", j=TILES)
+            width = TILES * IN // pieces
+            for i in range(pieces):
+                cols = slice(i * width, (i + 1) * width)
+                nc.sync.dma_start(out=x_sb[:, cols], in_=rows[:, cols])
+            return x_sb
+
+        x_tiles = [load_chunk(0, TILES)]
+        w_rows = []
+        for t in range(OUT_TILES):
+            w_rows.append(const.tile([P, IN + 2], BF16, name="w_rows%d" % t))
+            nc.sync.dma_start(out=w_rows[t][:, : IN + 1], in_=weight[t * P : (t + 1) * P, :])
+        for c in range(1, CHUNKS):
+            x_tiles.append(load_chunk(c, 1))
+
+        def transpose_rows(row_words, grouped_words):
+            xt = xt_pool.tile([P, ROW_WORDS], F32, name="xt")
+            for b in range(BLOCKS):
+                g, u = divmod(b, HALVES)
+                words = slice(g * P * HALVES + u, (g + 1) * P * HALVES, HALVES)
+                nc.tensor.transpose(xt[:, b * P : (b + 1) * P], row_words[:, words], ident_f32[:])
+            nc.scalar.copy(
+                out=grouped_words,
+                in_=xt[:].rearrange("p (g u r) -> p g r u", g=PASSES, u=HALVES),
+            )
+            return xt
+
+        def clear_signs(absolute, values):
+            nc.vector.tensor_single_scalar(
+                out=absolute.bitcast(I32),
+                in_=values.bitcast(I32),
+                scalar=SIGNLESS,
+                op=ALU.bitwise_and,
+            )
+
+        def quantise(operand, values):
+            codes, scales = operand
+            nc.vector.quantize_mx(out=codes[:].bitcast(FP8X4), scales=scales[:], in_=values[:])
+
+        w_signed = [
+            const.tile([P, PASSES * OUT], U32, name="w_codes", align_bytes=64),
+            const.tile([P, PASSES * OUT], U8, name="w_scales", align_bytes=64),
+        ]
+        w_absolute = [
+            const.tile([P, PASSES * OUT], U32, name="w_abs_codes", align_bytes=64),
+            const.tile([P, PASSES * OUT], U8, name="w_abs_scales", align_bytes=64),
+        ]
+        bias = const.tile([P, PAIR * OUT], F32)
+
+        w_grouped = const.tile([P, PASSES * OUT * PACK], BF16, align_bytes=64)
+        w_grouped_abs = const.tile([P, PASSES * OUT * PACK], BF16, align_bytes=64)
+
+        def transpose_weight():
+            w_grouped_words = w_grouped[:].bitcast(F32).rearrange(
+                "p (g o u) -> p g o u", g=PASSES, u=HALVES
+            )
+            for t in range(OUT_TILES):
+                transpose_rows(
+                    w_rows[t][:].bitcast(F32), w_grouped_words[:, :, t * P : (t + 1) * P, :]
+                )
+            bias_ps = acc_pool.tile([P, PAIR, OUT], F32, name="bias_ps", tag="acc")
+            for i in range(PAIR):
+                for t in range(OUT_TILES):
+                    nc.tensor.matmul(
+                        out=bias_ps[:, i, t * P : (t + 1) * P],
+                        lhsT=w_rows[t][:, IN : IN + 1].to_broadcast([P, P]),
+                        rhs=ident_bf16[:],
+                        start=True,
+                        stop=True,
+                    )
+            nc.scalar.activation(
+                out=bias[:], in_=bias_ps[:].rearrange("p i o -> p (i o)"), func=ACT.Relu
+            )
+
+        def quantise_weight():
+            clear_signs(w_grouped_abs[:], w_grouped[:])
+            quantise(w_signed, w_grouped)
+            quantise(w_absolute, w_grouped_abs)
+
+        grouped_of = {}
+        grouped_abs_of = {}
+        signed_of = {}
+        absolute_of = {}
+        acc_of = {}
+
+        def transpose_chunk(c):
+            grouped = grouped_pool.tile([P, TILES * IN], BF16, name="grouped", align_bytes=64)
+            grouped_words = grouped[:].bitcast(F32).rearrange(
+                "p (j g r u) -> p j g r u", j=TILES, g=PASSES, u=HALVES
+            )
+            grouped_abs = grouped_pool.tile(
+                [P, TILES * IN], BF16, name="grouped_abs", align_bytes=64
+            )
+            abs_values = grouped_abs[:].rearrange(
+                "p (j g r u e) -> p j g r u e", j=TILES, g=PASSES, u=HALVES, e=2
+            )
+            x_words = x_tiles[c][:].bitcast(F32)
+            for j in range(TILES):
+                xt = transpose_rows(
+                    x_words[:, j * ROW_WORDS : (j + 1) * ROW_WORDS], grouped_words[:, j]
+                )
+                if j >= VECTOR_ABS_TILES:
+                    xt_values = xt[:].bitcast(BF16).rearrange(
+                        "p (g u r e) -> p g r u e", g=PASSES, u=HALVES, e=2
+                    )
+                    for g in range(PASSES):
+                        nc.scalar.activation(
+                            out=abs_values[:, j, g], in_=xt_values[:, g], func=ACT.Abs
+                        )
+            grouped_of[c] = grouped
+            grouped_abs_of[c] = grouped_abs
+
+        def new_operand(kind):
+            width = TILES * PASSES * P
+            return [
+                codes_pool.tile([P, width], U32, name=kind + "_codes", align_bytes=64),
+                codes_pool.tile([P, width], U8, name=kind + "_scales", align_bytes=64),
+            ]
+
+        def clear_signs_of_chunk(c):
+            cols = slice(0, VECTOR_ABS_TILES * IN)
+            clear_signs(grouped_abs_of[c][:, cols], grouped_of[c][:, cols])
+
+        def quantise_signed(c):
+            signed_of[c] = new_operand("signed")
+            quantise(signed_of[c], grouped_of[c])
+
+        def quantise_absolute(c):
+            absolute_of[c] = new_operand("absolute")
+            quantise(absolute_of[c], grouped_abs_of[c])
+
+        def multiply_chunk(c):
+            acc_of[c] = []
+            for h in range(BANKS):
+                acc = acc_pool.tile([P, PAIR, OUT], F32, name="acc")
+                for i in range(PAIR):
+                    j = h * PAIR + i
+                    products = ((signed_of[c], w_signed), (absolute_of[c], w_absolute))
+                    for n, (x_operand, w_operand) in enumerate(products):
+                        for g in range(PASSES):
+                            rows = slice((j * PASSES + g) * P, (j * PASSES + g + 1) * P)
+                            cols = slice(g * OUT, (g + 1) * OUT)
+                            nc.tensor.matmul_mx(
+                                out=acc[:, i, :],
+                                lhsT=x_operand[0][:, rows].bitcast(FP8X4),
+                                lhsT_scale=x_operand[1][:, rows],
+                                rhs=w_operand[0][:, cols].bitcast(FP8X4),
+                                rhs_scale=w_operand[1][:, cols],
+                                start=(n == 0 and g == 0),
+                                stop=(n == 1 and g == PASSES - 1),
+                            )
+                acc_of[c].append(acc)
+
+        def finish_bank(c, h):
+            y = y_pool.tile([P, PAIR * OUT], F32, name="y")
+            nc.vector.scalar_tensor_tensor(
+                out=y[:],
+                in0=acc_of[c][h][:].rearrange("p i o -> p (i o)"),
+                scalar=0.5,
+                in1=bias[:],
+                op0=ALU.mult,
+                op1=ALU.add,
+            )
+            out_chunk = out[c * CHUNK : (c + 1) * CHUNK, :].rearrange("(p j) o -> p (j o)", j=TILES)
+            nc.sync.dma_start(out=out_chunk[:, h * PAIR * OUT : (h + 1) * PAIR * OUT], in_=y[:])
+
+        for s in range(CHUNKS + LAG):
+            if s < CHUNKS:
+                transpose_chunk(s)
+            if s == 0:
+                transpose_weight()
+            if s >= LAG:
+                multiply_chunk(s - LAG)
+            if s < CHUNKS:
+                clear_signs_of_chunk(s)
+                quantise_signed(s)
+            if s >= LAG:
+                finish_bank(s - LAG, 0)
+            if s < CHUNKS:
+                quantise_absolute(s)
+            if s >= LAG:
+                finish_bank(s - LAG, 1)
+            if s == 0:
+                quantise_weight()

@@ -28,6 +28,7 @@ CHUNK = TILES * P
 CHUNKS = TOKENS // CHUNK
 PAIR = 2
 BANKS = TILES // PAIR
+AHEAD = 7
 LAG = 2
 VECTOR_ABS_TILES = 2
 
@@ -42,7 +43,7 @@ def tile_skanlinear_t_kernel(tc, x, weight, out):
 
     with ExitStack() as stack:
         const = stack.enter_context(tc.tile_pool(name="const", bufs=1))
-        x_pool = stack.enter_context(tc.tile_pool(name="x", bufs=CHUNKS))
+        x_pool = stack.enter_context(tc.tile_pool(name="x", bufs=AHEAD + 1))
         grouped_pool = stack.enter_context(tc.tile_pool(name="grouped", bufs=2))
         codes_pool = stack.enter_context(tc.tile_pool(name="codes", bufs=LAG + 1))
         y_pool = stack.enter_context(tc.tile_pool(name="y", bufs=3 * BANKS))
@@ -69,7 +70,7 @@ def tile_skanlinear_t_kernel(tc, x, weight, out):
         for t in range(OUT_TILES):
             w_rows.append(const.tile([P, IN + 2], BF16, name="w_rows%d" % t))
             nc.sync.dma_start(out=w_rows[t][:, : IN + 1], in_=weight[t * P : (t + 1) * P, :])
-        for c in range(1, CHUNKS):
+        for c in range(1, AHEAD):
             x_tiles.append(load_chunk(c, 1))
 
         def transpose_rows(row_words, grouped_words):
@@ -241,3 +242,5 @@ def tile_skanlinear_t_kernel(tc, x, weight, out):
                 finish_bank(s - LAG, 1)
             if s == 0:
                 quantise_weight()
+            if s + AHEAD < CHUNKS:
+                x_tiles.append(load_chunk(s + AHEAD, 1))

@@ -30,7 +30,7 @@ PAIR = 2
 BANKS = TILES // PAIR
 AHEAD = 7
 LAG = 2
-VECTOR_ABS_TILES = 2
+SCALAR_ABS_TILES = 2
 
 SIGNLESS = 0x7FFF7FFF
 
@@ -83,7 +83,6 @@ def tile_skanlinear_t_kernel(tc, x, weight, out):
                 out=grouped_words,
                 in_=xt[:].rearrange("p (g u r) -> p g r u", g=PASSES, u=HALVES),
             )
-            return xt
 
         def clear_signs(absolute, values):
             nc.vector.tensor_single_scalar(
@@ -151,22 +150,11 @@ def tile_skanlinear_t_kernel(tc, x, weight, out):
             grouped_abs = grouped_pool.tile(
                 [P, TILES * IN], BF16, name="grouped_abs", align_bytes=64
             )
-            abs_values = grouped_abs[:].rearrange(
-                "p (j g r u e) -> p j g r u e", j=TILES, g=PASSES, u=HALVES, e=2
-            )
             x_words = x_tiles[c][:].bitcast(F32)
             for j in range(TILES):
-                xt = transpose_rows(
-                    x_words[:, j * ROW_WORDS : (j + 1) * ROW_WORDS], grouped_words[:, j]
-                )
-                if j >= VECTOR_ABS_TILES:
-                    xt_values = xt[:].bitcast(BF16).rearrange(
-                        "p (g u r e) -> p g r u e", g=PASSES, u=HALVES, e=2
-                    )
-                    for g in range(PASSES):
-                        nc.scalar.activation(
-                            out=abs_values[:, j, g], in_=xt_values[:, g], func=ACT.Abs
-                        )
+                transpose_rows(x_words[:, j * ROW_WORDS : (j + 1) * ROW_WORDS], grouped_words[:, j])
+            cols = slice(0, SCALAR_ABS_TILES * IN)
+            nc.scalar.activation(out=grouped_abs[:, cols], in_=grouped[:, cols], func=ACT.Abs)
             grouped_of[c] = grouped
             grouped_abs_of[c] = grouped_abs
 
@@ -178,7 +166,7 @@ def tile_skanlinear_t_kernel(tc, x, weight, out):
             ]
 
         def clear_signs_of_chunk(c):
-            cols = slice(0, VECTOR_ABS_TILES * IN)
+            cols = slice(SCALAR_ABS_TILES * IN, TILES * IN)
             clear_signs(grouped_abs_of[c][:, cols], grouped_of[c][:, cols])
 
         def quantise_signed(c):

@@ -66,11 +66,12 @@ def tile_skanlinear_t_kernel(tc, x, weight, out):
             return x_sb
 
         x_tiles = [load_chunk(0, TILES)]
+        x_tiles.append(load_chunk(1, TILES))
         w_rows = []
         for t in range(OUT_TILES):
             w_rows.append(const.tile([P, IN + 2], BF16, name="w_rows%d" % t))
             nc.sync.dma_start(out=w_rows[t][:, : IN + 1], in_=weight[t * P : (t + 1) * P, :])
-        for c in range(1, AHEAD):
+        for c in range(2, AHEAD):
             x_tiles.append(load_chunk(c, 1))
 
         def transpose_rows(row_words, grouped_words):
@@ -136,6 +137,9 @@ def tile_skanlinear_t_kernel(tc, x, weight, out):
             quantise(w_signed, w_grouped)
             quantise(w_absolute, w_grouped_abs)
 
+        def scalar_abs_tiles(c):
+            return 0 if c < LAG else SCALAR_ABS_TILES
+
         grouped_of = {}
         grouped_abs_of = {}
         signed_of = {}
@@ -153,8 +157,9 @@ def tile_skanlinear_t_kernel(tc, x, weight, out):
             x_words = x_tiles[c][:].bitcast(F32)
             for j in range(TILES):
                 transpose_rows(x_words[:, j * ROW_WORDS : (j + 1) * ROW_WORDS], grouped_words[:, j])
-            cols = slice(0, SCALAR_ABS_TILES * IN)
-            nc.scalar.activation(out=grouped_abs[:, cols], in_=grouped[:, cols], func=ACT.Abs)
+            if scalar_abs_tiles(c):
+                cols = slice(0, scalar_abs_tiles(c) * IN)
+                nc.scalar.activation(out=grouped_abs[:, cols], in_=grouped[:, cols], func=ACT.Abs)
             grouped_of[c] = grouped
             grouped_abs_of[c] = grouped_abs
 
@@ -166,7 +171,7 @@ def tile_skanlinear_t_kernel(tc, x, weight, out):
             ]
 
         def clear_signs_of_chunk(c):
-            cols = slice(SCALAR_ABS_TILES * IN, TILES * IN)
+            cols = slice(scalar_abs_tiles(c) * IN, TILES * IN)
             clear_signs(grouped_abs_of[c][:, cols], grouped_of[c][:, cols])
 
         def quantise_signed(c):
@@ -215,8 +220,9 @@ def tile_skanlinear_t_kernel(tc, x, weight, out):
         for s in range(CHUNKS + LAG):
             if s < CHUNKS:
                 transpose_chunk(s)
-            if s == 0:
+            if s == 1:
                 transpose_weight()
+                quantise_weight()
             if s >= LAG:
                 multiply_chunk(s - LAG)
             if s < CHUNKS:
@@ -228,7 +234,5 @@ def tile_skanlinear_t_kernel(tc, x, weight, out):
                 quantise_absolute(s)
             if s >= LAG:
                 finish_bank(s - LAG, 1)
-            if s == 0:
-                quantise_weight()
             if s + AHEAD < CHUNKS:
                 x_tiles.append(load_chunk(s + AHEAD, 1))

@@ -32,6 +32,8 @@ AHEAD = 7
 LAG = 2
 SCALAR_ABS_TILES = 2
 
+SORTED_TILES = 1
+
 SIGNLESS = 0x7FFF7FFF
 
 FLOPS = 2 * 2 * TOKENS * IN * OUT
@@ -43,10 +45,11 @@ def tile_skanlinear_t_kernel(tc, x, weight, out):
 
     with ExitStack() as stack:
         const = stack.enter_context(tc.tile_pool(name="const", bufs=1))
+        sorted_pool = stack.enter_context(tc.tile_pool(name="sorted", bufs=2))
         x_pool = stack.enter_context(tc.tile_pool(name="x", bufs=AHEAD + 1))
         grouped_pool = stack.enter_context(tc.tile_pool(name="grouped", bufs=2))
         codes_pool = stack.enter_context(tc.tile_pool(name="codes", bufs=LAG + 1))
-        y_pool = stack.enter_context(tc.tile_pool(name="y", bufs=3 * BANKS))
+        y_pool = stack.enter_context(tc.tile_pool(name="y", bufs=5 * BANKS))
         xt_pool = stack.enter_context(tc.psum_pool(name="xt", bufs=4))
         acc_pool = stack.enter_context(tc.psum_pool(name="acc", bufs=4))
         stack.enter_context(tc.manual_schedule())
@@ -71,14 +74,18 @@ def tile_skanlinear_t_kernel(tc, x, weight, out):
         for t in range(OUT_TILES):
             w_rows.append(const.tile([P, IN + 2], BF16, name="w_rows%d" % t))
             nc.sync.dma_start(out=w_rows[t][:, : IN + 1], in_=weight[t * P : (t + 1) * P, :])
-        for c in range(2, AHEAD):
+        x_tiles.append(load_chunk(2, TILES))
+        for c in range(3, AHEAD):
             x_tiles.append(load_chunk(c, 1))
 
-        def transpose_rows(row_words, grouped_words):
+        def transpose_rows(row_words, grouped_words, is_sorted=False):
             xt = xt_pool.tile([P, ROW_WORDS], F32, name="xt")
             for b in range(BLOCKS):
                 g, u = divmod(b, HALVES)
-                words = slice(g * P * HALVES + u, (g + 1) * P * HALVES, HALVES)
+                if is_sorted:
+                    words = slice(b * P, (b + 1) * P)
+                else:
+                    words = slice(g * P * HALVES + u, (g + 1) * P * HALVES, HALVES)
                 nc.tensor.transpose(xt[:, b * P : (b + 1) * P], row_words[:, words], ident_f32[:])
             nc.scalar.copy(
                 out=grouped_words,
@@ -140,11 +147,25 @@ def tile_skanlinear_t_kernel(tc, x, weight, out):
         def scalar_abs_tiles(c):
             return 0 if c < LAG else SCALAR_ABS_TILES
 
+        sorted_of = {}
         grouped_of = {}
         grouped_abs_of = {}
         signed_of = {}
         absolute_of = {}
         acc_of = {}
+
+        def first_sorted(c):
+            return TILES if c < LAG else TILES - SORTED_TILES
+
+        def sort_words(c):
+            words = sorted_pool.tile([P, SORTED_TILES * ROW_WORDS], F32, name="sorted_words")
+            nc.vector.tensor_copy(
+                out=words[:].rearrange("p (b u i) -> p b u i", u=HALVES, i=P),
+                in_=x_tiles[c][:]
+                .bitcast(F32)[:, first_sorted(c) * ROW_WORDS :]
+                .rearrange("p (b i u) -> p b u i", u=HALVES, i=P),
+            )
+            sorted_of[c] = words
 
         def transpose_chunk(c):
             grouped = grouped_pool.tile([P, TILES * IN], BF16, name="grouped", align_bytes=64)
@@ -156,7 +177,12 @@ def tile_skanlinear_t_kernel(tc, x, weight, out):
             )
             x_words = x_tiles[c][:].bitcast(F32)
             for j in range(TILES):
-                transpose_rows(x_words[:, j * ROW_WORDS : (j + 1) * ROW_WORDS], grouped_words[:, j])
+                if j < first_sorted(c):
+                    row_words = x_words[:, j * ROW_WORDS : (j + 1) * ROW_WORDS]
+                else:
+                    at = (j - first_sorted(c)) * ROW_WORDS
+                    row_words = sorted_of[c][:, at : at + ROW_WORDS]
+                transpose_rows(row_words, grouped_words[:, j], j >= first_sorted(c))
             if scalar_abs_tiles(c):
                 cols = slice(0, scalar_abs_tiles(c) * IN)
                 nc.scalar.activation(out=grouped_abs[:, cols], in_=grouped[:, cols], func=ACT.Abs)
@@ -182,12 +208,15 @@ def tile_skanlinear_t_kernel(tc, x, weight, out):
             absolute_of[c] = new_operand("absolute")
             quantise(absolute_of[c], grouped_abs_of[c])
 
+        def share(c):
+            return PAIR if c < CHUNKS - 1 else 1
+
         def multiply_chunk(c):
             acc_of[c] = []
-            for h in range(BANKS):
+            for h in range(TILES // share(c)):
                 acc = acc_pool.tile([P, PAIR, OUT], F32, name="acc")
-                for i in range(PAIR):
-                    j = h * PAIR + i
+                for i in range(share(c)):
+                    j = h * share(c) + i
                     products = ((signed_of[c], w_signed), (absolute_of[c], w_absolute))
                     for n, (x_operand, w_operand) in enumerate(products):
                         for g in range(PASSES):
@@ -205,17 +234,18 @@ def tile_skanlinear_t_kernel(tc, x, weight, out):
                 acc_of[c].append(acc)
 
         def finish_bank(c, h):
+            width = share(c) * OUT
             y = y_pool.tile([P, PAIR * OUT], F32, name="y")
             nc.vector.scalar_tensor_tensor(
-                out=y[:],
-                in0=acc_of[c][h][:].rearrange("p i o -> p (i o)"),
+                out=y[:, :width],
+                in0=acc_of[c][h][:].rearrange("p i o -> p (i o)")[:, :width],
                 scalar=0.5,
-                in1=bias[:],
+                in1=bias[:, :width],
                 op0=ALU.mult,
                 op1=ALU.add,
             )
             out_chunk = out[c * CHUNK : (c + 1) * CHUNK, :].rearrange("(p j) o -> p (j o)", j=TILES)
-            nc.sync.dma_start(out=out_chunk[:, h * PAIR * OUT : (h + 1) * PAIR * OUT], in_=y[:])
+            nc.sync.dma_start(out=out_chunk[:, h * width : (h + 1) * width], in_=y[:, :width])
 
         for s in range(CHUNKS + LAG):
             if s < CHUNKS:
@@ -233,6 +263,9 @@ def tile_skanlinear_t_kernel(tc, x, weight, out):
             if s < CHUNKS:
                 quantise_absolute(s)
             if s >= LAG:
-                finish_bank(s - LAG, 1)
+                for h in range(1, TILES // share(s - LAG)):
+                    finish_bank(s - LAG, h)
+            if s + 1 < CHUNKS and first_sorted(s + 1) < TILES:
+                sort_words(s + 1)
             if s + AHEAD < CHUNKS:
                 x_tiles.append(load_chunk(s + AHEAD, 1))

@@ -45,7 +45,7 @@ def tile_skanlinear_t_kernel(tc, x, weight, out):
 
     with ExitStack() as stack:
         const = stack.enter_context(tc.tile_pool(name="const", bufs=1))
-        sorted_pool = stack.enter_context(tc.tile_pool(name="sorted", bufs=2))
+        sorted_pool = stack.enter_context(tc.tile_pool(name="sorted", bufs=LAG + 1))
         x_pool = stack.enter_context(tc.tile_pool(name="x", bufs=AHEAD + 1))
         grouped_pool = stack.enter_context(tc.tile_pool(name="grouped", bufs=2))
         codes_pool = stack.enter_context(tc.tile_pool(name="codes", bufs=LAG + 1))
@@ -260,12 +260,12 @@ def tile_skanlinear_t_kernel(tc, x, weight, out):
                 quantise_signed(s)
             if s >= LAG:
                 finish_bank(s - LAG, 0)
+            if s + LAG < CHUNKS:
+                sort_words(s + LAG)
             if s < CHUNKS:
                 quantise_absolute(s)
             if s >= LAG:
                 for h in range(1, TILES // share(s - LAG)):
                     finish_bank(s - LAG, h)
-            if s + 1 < CHUNKS and first_sorted(s + 1) < TILES:
-                sort_words(s + 1)
             if s + AHEAD < CHUNKS:
                 x_tiles.append(load_chunk(s + AHEAD, 1))

@@ -30,7 +30,7 @@ PAIR = 2
 BANKS = TILES // PAIR
 AHEAD = 7
 LAG = 2
-SCALAR_ABS_TILES = 2
+SCALAR_ABS_TILES = 1.5
 
 SORTED_TILES = 1
 
@@ -47,7 +47,7 @@ def tile_skanlinear_t_kernel(tc, x, weight, out):
         const = stack.enter_context(tc.tile_pool(name="const", bufs=1))
         sorted_pool = stack.enter_context(tc.tile_pool(name="sorted", bufs=LAG + 1))
         x_pool = stack.enter_context(tc.tile_pool(name="x", bufs=AHEAD + 1))
-        grouped_pool = stack.enter_context(tc.tile_pool(name="grouped", bufs=2))
+        grouped_pool = stack.enter_context(tc.tile_pool(name="grouped", bufs=3))
         codes_pool = stack.enter_context(tc.tile_pool(name="codes", bufs=LAG + 1))
         y_pool = stack.enter_context(tc.tile_pool(name="y", bufs=5 * BANKS))
         xt_pool = stack.enter_context(tc.psum_pool(name="xt", bufs=4))
@@ -144,8 +144,8 @@ def tile_skanlinear_t_kernel(tc, x, weight, out):
             quantise(w_signed, w_grouped)
             quantise(w_absolute, w_grouped_abs)
 
-        def scalar_abs_tiles(c):
-            return 0 if c < LAG else SCALAR_ABS_TILES
+        def scalar_abs_cols(c):
+            return 0 if c < LAG else int(SCALAR_ABS_TILES * IN)
 
         sorted_of = {}
         grouped_of = {}
@@ -155,11 +155,11 @@ def tile_skanlinear_t_kernel(tc, x, weight, out):
         acc_of = {}
 
         def first_sorted(c):
-            return TILES if c < LAG else TILES - SORTED_TILES
+            return TILES if c < 2 * LAG else TILES - SORTED_TILES
 
         def sort_words(c):
             words = sorted_pool.tile([P, SORTED_TILES * ROW_WORDS], F32, name="sorted_words")
-            nc.vector.tensor_copy(
+            nc.scalar.copy(
                 out=words[:].rearrange("p (b u i) -> p b u i", u=HALVES, i=P),
                 in_=x_tiles[c][:]
                 .bitcast(F32)[:, first_sorted(c) * ROW_WORDS :]
@@ -183,8 +183,8 @@ def tile_skanlinear_t_kernel(tc, x, weight, out):
                     at = (j - first_sorted(c)) * ROW_WORDS
                     row_words = sorted_of[c][:, at : at + ROW_WORDS]
                 transpose_rows(row_words, grouped_words[:, j], j >= first_sorted(c))
-            if scalar_abs_tiles(c):
-                cols = slice(0, scalar_abs_tiles(c) * IN)
+            if scalar_abs_cols(c):
+                cols = slice(0, scalar_abs_cols(c))
                 nc.scalar.activation(out=grouped_abs[:, cols], in_=grouped[:, cols], func=ACT.Abs)
             grouped_of[c] = grouped
             grouped_abs_of[c] = grouped_abs
@@ -197,8 +197,12 @@ def tile_skanlinear_t_kernel(tc, x, weight, out):
             ]
 
         def clear_signs_of_chunk(c):
-            cols = slice(scalar_abs_tiles(c) * IN, TILES * IN)
-            clear_signs(grouped_abs_of[c][:, cols], grouped_of[c][:, cols])
+            pieces = TILES if c == 0 else 1
+            start = scalar_abs_cols(c)
+            width = (TILES * IN - start) // pieces
+            for i in range(pieces):
+                cols = slice(start + i * width, start + (i + 1) * width)
+                clear_signs(grouped_abs_of[c][:, cols], grouped_of[c][:, cols])
 
         def quantise_signed(c):
             signed_of[c] = new_operand("signed")
@@ -250,6 +254,8 @@ def tile_skanlinear_t_kernel(tc, x, weight, out):
         for s in range(CHUNKS + LAG):
             if s < CHUNKS:
                 transpose_chunk(s)
+            if LAG <= s < CHUNKS - LAG:
+                sort_words(s + LAG)
             if s == 1:
                 transpose_weight()
                 quantise_weight()
@@ -260,8 +266,6 @@ def tile_skanlinear_t_kernel(tc, x, weight, out):
                 quantise_signed(s)
             if s >= LAG:
                 finish_bank(s - LAG, 0)
-            if s + LAG < CHUNKS:
-                sort_words(s + LAG)
             if s < CHUNKS:
                 quantise_absolute(s)
             if s >= LAG:

@@ -28,9 +28,11 @@ CHUNK = TILES * P
 CHUNKS = TOKENS // CHUNK
 PAIR = 2
 BANKS = TILES // PAIR
-AHEAD = 7
+AHEAD = 6
 LAG = 2
 SCALAR_ABS_TILES = 1.5
+LATE_ABS_TILES = 2
+LAST_ABS_TILES = 3
 
 SORTED_TILES = 1
 
@@ -49,7 +51,7 @@ def tile_skanlinear_t_kernel(tc, x, weight, out):
         x_pool = stack.enter_context(tc.tile_pool(name="x", bufs=AHEAD + 1))
         grouped_pool = stack.enter_context(tc.tile_pool(name="grouped", bufs=3))
         codes_pool = stack.enter_context(tc.tile_pool(name="codes", bufs=LAG + 1))
-        y_pool = stack.enter_context(tc.tile_pool(name="y", bufs=5 * BANKS))
+        y_pool = stack.enter_context(tc.tile_pool(name="y", bufs=(CHUNKS - 1) * BANKS + TILES))
         xt_pool = stack.enter_context(tc.psum_pool(name="xt", bufs=4))
         acc_pool = stack.enter_context(tc.psum_pool(name="acc", bufs=4))
         stack.enter_context(tc.manual_schedule())
@@ -69,11 +71,11 @@ def tile_skanlinear_t_kernel(tc, x, weight, out):
             return x_sb
 
         x_tiles = [load_chunk(0, TILES)]
-        x_tiles.append(load_chunk(1, TILES))
         w_rows = []
         for t in range(OUT_TILES):
             w_rows.append(const.tile([P, IN + 2], BF16, name="w_rows%d" % t))
             nc.sync.dma_start(out=w_rows[t][:, : IN + 1], in_=weight[t * P : (t + 1) * P, :])
+        x_tiles.append(load_chunk(1, TILES))
         x_tiles.append(load_chunk(2, TILES))
         for c in range(3, AHEAD):
             x_tiles.append(load_chunk(c, 1))
@@ -125,6 +127,8 @@ def tile_skanlinear_t_kernel(tc, x, weight, out):
                 transpose_rows(
                     w_rows[t][:].bitcast(F32), w_grouped_words[:, :, t * P : (t + 1) * P, :]
                 )
+
+        def spread_bias():
             bias_ps = acc_pool.tile([P, PAIR, OUT], F32, name="bias_ps", tag="acc")
             for i in range(PAIR):
                 for t in range(OUT_TILES):
@@ -145,7 +149,9 @@ def tile_skanlinear_t_kernel(tc, x, weight, out):
             quantise(w_absolute, w_grouped_abs)
 
         def scalar_abs_cols(c):
-            return 0 if c < LAG else int(SCALAR_ABS_TILES * IN)
+            if c < LAG:
+                return 0
+            return int((SCALAR_ABS_TILES, LATE_ABS_TILES, LAST_ABS_TILES)[max(0, c - CHUNKS + 3)] * IN)
 
         sorted_of = {}
         grouped_of = {}
@@ -184,8 +190,13 @@ def tile_skanlinear_t_kernel(tc, x, weight, out):
                     row_words = sorted_of[c][:, at : at + ROW_WORDS]
                 transpose_rows(row_words, grouped_words[:, j], j >= first_sorted(c))
             if scalar_abs_cols(c):
-                cols = slice(0, scalar_abs_cols(c))
-                nc.scalar.activation(out=grouped_abs[:, cols], in_=grouped[:, cols], func=ACT.Abs)
+                ends = [scalar_abs_cols(c)] if c < CHUNKS - 1 else [PAIR * IN, scalar_abs_cols(c)]
+                start = 0
+                for end in ends:
+                    nc.scalar.activation(
+                        out=grouped_abs[:, start:end], in_=grouped[:, start:end], func=ACT.Abs
+                    )
+                    start = end
             grouped_of[c] = grouped
             grouped_abs_of[c] = grouped_abs
 
@@ -197,12 +208,30 @@ def tile_skanlinear_t_kernel(tc, x, weight, out):
             ]
 
         def clear_signs_of_chunk(c):
-            pieces = TILES if c == 0 else 1
-            start = scalar_abs_cols(c)
-            width = (TILES * IN - start) // pieces
-            for i in range(pieces):
-                cols = slice(start + i * width, start + (i + 1) * width)
-                clear_signs(grouped_abs_of[c][:, cols], grouped_of[c][:, cols])
+            cols = slice(scalar_abs_cols(c), TILES * IN)
+            clear_signs(grouped_abs_of[c][:, cols], grouped_of[c][:, cols])
+
+        def quantise_by_blocks(c):
+            signed_of[c] = new_operand("signed")
+            absolute_of[c] = new_operand("absolute")
+
+            def part(operand, values, j):
+                codes, scales = operand
+                words = slice(j * PASSES * P, (j + 1) * PASSES * P)
+                nc.vector.quantize_mx(
+                    out=codes[:, words].bitcast(FP8X4),
+                    scales=scales[:, words],
+                    in_=values[:, j * IN : (j + 1) * IN],
+                )
+
+            for j in range(TILES + 1):
+                if j < TILES:
+                    cols = slice(j * IN, (j + 1) * IN)
+                    clear_signs(grouped_abs_of[c][:, cols], grouped_of[c][:, cols])
+                if j > 0:
+                    part(absolute_of[c], grouped_abs_of[c], j - 1)
+                if j < TILES:
+                    part(signed_of[c], grouped_of[c], j)
 
         def quantise_signed(c):
             signed_of[c] = new_operand("signed")
@@ -210,32 +239,53 @@ def tile_skanlinear_t_kernel(tc, x, weight, out):
 
         def quantise_absolute(c):
             absolute_of[c] = new_operand("absolute")
-            quantise(absolute_of[c], grouped_abs_of[c])
+            halves = 1 if c < CHUNKS - 1 else 2
+            codes, scales = absolute_of[c]
+            width = TILES * PASSES * P // halves
+            for i in range(halves):
+                words = slice(i * width, (i + 1) * width)
+                nc.vector.quantize_mx(
+                    out=codes[:, words].bitcast(FP8X4),
+                    scales=scales[:, words],
+                    in_=grouped_abs_of[c][:, i * width * PACK : (i + 1) * width * PACK],
+                )
 
         def share(c):
             return PAIR if c < CHUNKS - 1 else 1
 
         def multiply_chunk(c):
+            products = ((signed_of[c], w_signed), (absolute_of[c], w_absolute))
+
+            def multiply_block(j, n):
+                x_operand, w_operand = products[n]
+                for g in range(PASSES):
+                    rows = slice((j * PASSES + g) * P, (j * PASSES + g + 1) * P)
+                    cols = slice(g * OUT, (g + 1) * OUT)
+                    nc.tensor.matmul_mx(
+                        out=acc_of[c][j // share(c)][:, j % share(c), :],
+                        lhsT=x_operand[0][:, rows].bitcast(FP8X4),
+                        lhsT_scale=x_operand[1][:, rows],
+                        rhs=w_operand[0][:, cols].bitcast(FP8X4),
+                        rhs_scale=w_operand[1][:, cols],
+                        start=(n == 0 and g == 0),
+                        stop=(n == 1 and g == PASSES - 1),
+                    )
+
             acc_of[c] = []
-            for h in range(TILES // share(c)):
-                acc = acc_pool.tile([P, PAIR, OUT], F32, name="acc")
-                for i in range(share(c)):
-                    j = h * share(c) + i
-                    products = ((signed_of[c], w_signed), (absolute_of[c], w_absolute))
-                    for n, (x_operand, w_operand) in enumerate(products):
-                        for g in range(PASSES):
-                            rows = slice((j * PASSES + g) * P, (j * PASSES + g + 1) * P)
-                            cols = slice(g * OUT, (g + 1) * OUT)
-                            nc.tensor.matmul_mx(
-                                out=acc[:, i, :],
-                                lhsT=x_operand[0][:, rows].bitcast(FP8X4),
-                                lhsT_scale=x_operand[1][:, rows],
-                                rhs=w_operand[0][:, cols].bitcast(FP8X4),
-                                rhs_scale=w_operand[1][:, cols],
-                                start=(n == 0 and g == 0),
-                                stop=(n == 1 and g == PASSES - 1),
-                            )
-                acc_of[c].append(acc)
+            if c < CHUNKS - 1:
+                for j in range(TILES):
+                    if j % share(c) == 0:
+                        acc = acc_pool.tile([P, PAIR, OUT], F32, name="acc")
+                        acc_of[c].append(acc)
+                    multiply_block(j, 0)
+                    multiply_block(j, 1)
+            else:
+                for j in range(TILES):
+                    acc = xt_pool.tile([P, PAIR, OUT], F32, name="last_acc", tag="xt")
+                    acc_of[c].append(acc)
+                    multiply_block(j, 0)
+                for j in range(TILES):
+                    multiply_block(j, 1)
 
         def finish_bank(c, h):
             width = share(c) * OUT
@@ -256,20 +306,25 @@ def tile_skanlinear_t_kernel(tc, x, weight, out):
                 transpose_chunk(s)
             if LAG <= s < CHUNKS - LAG:
                 sort_words(s + LAG)
-            if s == 1:
+            if s == 0:
                 transpose_weight()
-                quantise_weight()
+            if s == 1:
+                spread_bias()
             if s >= LAG:
                 multiply_chunk(s - LAG)
-            if s < CHUNKS:
+            if s == 0:
+                quantise_by_blocks(s)
+                quantise_weight()
+            elif s < CHUNKS:
                 clear_signs_of_chunk(s)
                 quantise_signed(s)
-            if s >= LAG:
-                finish_bank(s - LAG, 0)
-            if s < CHUNKS:
+            finished = TILES // share(s - LAG) if s >= LAG else 0
+            before = min(finished, 1) if s < CHUNKS - 1 else finished
+            for h in range(before):
+                finish_bank(s - LAG, h)
+            if 0 < s < CHUNKS:
                 quantise_absolute(s)
-            if s >= LAG:
-                for h in range(1, TILES // share(s - LAG)):
-                    finish_bank(s - LAG, h)
+            for h in range(before, finished):
+                finish_bank(s - LAG, h)
             if s + AHEAD < CHUNKS:
                 x_tiles.append(load_chunk(s + AHEAD, 1))

@@ -30,7 +30,7 @@ PAIR = 2
 BANKS = TILES // PAIR
 AHEAD = 6
 LAG = 2
-SCALAR_ABS_TILES = 1.5
+SCALAR_ABS_TILES = 1.25
 LATE_ABS_TILES = 2
 LAST_ABS_TILES = 3
 

@@ -30,9 +30,8 @@ PAIR = 2
 BANKS = TILES // PAIR
 AHEAD = 6
 LAG = 2
-SCALAR_ABS_TILES = 1.25
+SCALAR_ABS_TILES = 1.375
 LATE_ABS_TILES = 2
-LAST_ABS_TILES = 3
 
 SORTED_TILES = 1
 
@@ -56,13 +55,13 @@ def tile_skanlinear_t_kernel(tc, x, weight, out):
         acc_pool = stack.enter_context(tc.psum_pool(name="acc", bufs=4))
         stack.enter_context(tc.manual_schedule())
 
-        ident_f32 = const.tile([P, P], F32)
+        ident_f32 = const.tile([P, P], F32, align_bytes=256)
         make_identity(nc, ident_f32[:])
         ident_bf16 = const.tile([P, P], BF16)
         make_identity(nc, ident_bf16[:])
 
         def load_chunk(c, pieces):
-            x_sb = x_pool.tile([P, TILES * IN], BF16, name="x_sb")
+            x_sb = x_pool.tile([P, TILES * IN], BF16, name="x_sb", align_bytes=256)
             rows = x_rows[c * CHUNK : (c + 1) * CHUNK, :].rearrange("(p j) k -> p (j k)", j=TILES)
             width = TILES * IN // pieces
             for i in range(pieces):
@@ -73,7 +72,7 @@ def tile_skanlinear_t_kernel(tc, x, weight, out):
         x_tiles = [load_chunk(0, TILES)]
         w_rows = []
         for t in range(OUT_TILES):
-            w_rows.append(const.tile([P, IN + 2], BF16, name="w_rows%d" % t))
+            w_rows.append(const.tile([P, IN + 2], BF16, name="w_rows%d" % t, align_bytes=256))
             nc.sync.dma_start(out=w_rows[t][:, : IN + 1], in_=weight[t * P : (t + 1) * P, :])
         x_tiles.append(load_chunk(1, TILES))
         x_tiles.append(load_chunk(2, TILES))
@@ -107,17 +106,17 @@ def tile_skanlinear_t_kernel(tc, x, weight, out):
             nc.vector.quantize_mx(out=codes[:].bitcast(FP8X4), scales=scales[:], in_=values[:])
 
         w_signed = [
-            const.tile([P, PASSES * OUT], U32, name="w_codes", align_bytes=64),
-            const.tile([P, PASSES * OUT], U8, name="w_scales", align_bytes=64),
+            const.tile([P, PASSES * OUT], U32, name="w_codes", align_bytes=256),
+            const.tile([P, PASSES * OUT], U8, name="w_scales", align_bytes=256),
         ]
         w_absolute = [
-            const.tile([P, PASSES * OUT], U32, name="w_abs_codes", align_bytes=64),
-            const.tile([P, PASSES * OUT], U8, name="w_abs_scales", align_bytes=64),
+            const.tile([P, PASSES * OUT], U32, name="w_abs_codes", align_bytes=256),
+            const.tile([P, PASSES * OUT], U8, name="w_abs_scales", align_bytes=256),
         ]
         bias = const.tile([P, PAIR * OUT], F32)
 
-        w_grouped = const.tile([P, PASSES * OUT * PACK], BF16, align_bytes=64)
-        w_grouped_abs = const.tile([P, PASSES * OUT * PACK], BF16, align_bytes=64)
+        w_grouped = const.tile([P, PASSES * OUT * PACK], BF16, align_bytes=256)
+        w_grouped_abs = const.tile([P, PASSES * OUT * PACK], BF16, align_bytes=256)
 
         def transpose_weight():
             w_grouped_words = w_grouped[:].bitcast(F32).rearrange(
@@ -151,7 +150,7 @@ def tile_skanlinear_t_kernel(tc, x, weight, out):
         def scalar_abs_cols(c):
             if c < LAG:
                 return 0
-            return int((SCALAR_ABS_TILES, LATE_ABS_TILES, LAST_ABS_TILES)[max(0, c - CHUNKS + 3)] * IN)
+            return int((SCALAR_ABS_TILES if c < CHUNKS - LAG else LATE_ABS_TILES) * IN)
 
         sorted_of = {}
         grouped_of = {}
@@ -164,7 +163,7 @@ def tile_skanlinear_t_kernel(tc, x, weight, out):
             return TILES if c < 2 * LAG else TILES - SORTED_TILES
 
         def sort_words(c):
-            words = sorted_pool.tile([P, SORTED_TILES * ROW_WORDS], F32, name="sorted_words")
+            words = sorted_pool.tile([P, SORTED_TILES * ROW_WORDS], F32, name="sorted_words", align_bytes=256)
             nc.scalar.copy(
                 out=words[:].rearrange("p (b u i) -> p b u i", u=HALVES, i=P),
                 in_=x_tiles[c][:]
@@ -174,12 +173,12 @@ def tile_skanlinear_t_kernel(tc, x, weight, out):
             sorted_of[c] = words
 
         def transpose_chunk(c):
-            grouped = grouped_pool.tile([P, TILES * IN], BF16, name="grouped", align_bytes=64)
+            grouped = grouped_pool.tile([P, TILES * IN], BF16, name="grouped", align_bytes=256)
             grouped_words = grouped[:].bitcast(F32).rearrange(
                 "p (j g r u) -> p j g r u", j=TILES, g=PASSES, u=HALVES
             )
             grouped_abs = grouped_pool.tile(
-                [P, TILES * IN], BF16, name="grouped_abs", align_bytes=64
+                [P, TILES * IN], BF16, name="grouped_abs", align_bytes=256
             )
             x_words = x_tiles[c][:].bitcast(F32)
             for j in range(TILES):
@@ -190,21 +189,16 @@ def tile_skanlinear_t_kernel(tc, x, weight, out):
                     row_words = sorted_of[c][:, at : at + ROW_WORDS]
                 transpose_rows(row_words, grouped_words[:, j], j >= first_sorted(c))
             if scalar_abs_cols(c):
-                ends = [scalar_abs_cols(c)] if c < CHUNKS - 1 else [PAIR * IN, scalar_abs_cols(c)]
-                start = 0
-                for end in ends:
-                    nc.scalar.activation(
-                        out=grouped_abs[:, start:end], in_=grouped[:, start:end], func=ACT.Abs
-                    )
-                    start = end
+                cols = slice(0, scalar_abs_cols(c))
+                nc.scalar.activation(out=grouped_abs[:, cols], in_=grouped[:, cols], func=ACT.Abs)
             grouped_of[c] = grouped
             grouped_abs_of[c] = grouped_abs
 
         def new_operand(kind):
             width = TILES * PASSES * P
             return [
-                codes_pool.tile([P, width], U32, name=kind + "_codes", align_bytes=64),
-                codes_pool.tile([P, width], U8, name=kind + "_scales", align_bytes=64),
+                codes_pool.tile([P, width], U32, name=kind + "_codes", align_bytes=256),
+                codes_pool.tile([P, width], U8, name=kind + "_scales", align_bytes=256),
             ]
 
         def clear_signs_of_chunk(c):
@@ -290,14 +284,21 @@ def tile_skanlinear_t_kernel(tc, x, weight, out):
         def finish_bank(c, h):
             width = share(c) * OUT
             y = y_pool.tile([P, PAIR * OUT], F32, name="y")
-            nc.vector.scalar_tensor_tensor(
-                out=y[:, :width],
-                in0=acc_of[c][h][:].rearrange("p i o -> p (i o)")[:, :width],
-                scalar=0.5,
-                in1=bias[:, :width],
-                op0=ALU.mult,
-                op1=ALU.add,
-            )
+            sums = acc_of[c][h][:].rearrange("p i o -> p (i o)")[:, :width]
+            if (c, h) == (CHUNKS - 1, 0):
+                nc.scalar.mul(y[:, :width], sums, 0.5)
+                nc.gpsimd.tensor_tensor(
+                    out=y[:, :width], in0=y[:, :width], in1=bias[:, :width], op=ALU.add
+                )
+            else:
+                nc.vector.scalar_tensor_tensor(
+                    out=y[:, :width],
+                    in0=sums,
+                    scalar=0.5,
+                    in1=bias[:, :width],
+                    op0=ALU.mult,
+                    op1=ALU.add,
+                )
             out_chunk = out[c * CHUNK : (c + 1) * CHUNK, :].rearrange("(p j) o -> p (j o)", j=TILES)
             nc.sync.dma_start(out=out_chunk[:, h * width : (h + 1) * width], in_=y[:, :width])
 

from contextlib import ExitStack

import concourse.mybir as mybir
from concourse.masks import make_identity

F32 = mybir.dt.float32
BF16 = mybir.dt.bfloat16
I32 = mybir.dt.int32
U32 = mybir.dt.uint32
U8 = mybir.dt.uint8
FP8X4 = mybir.dt.float8_e4m3fn_x4
ALU = mybir.AluOpType
ACT = mybir.ActivationFunctionType

P = 128
TOKENS = 8192
IN = 1024
OUT = 256
PACK = 4
PASSES = IN // (P * PACK)
HALVES = 2
ROW_WORDS = IN // 2
BLOCKS = ROW_WORDS // P
OUT_TILES = OUT // P

TILES = 4
CHUNK = TILES * P
CHUNKS = TOKENS // CHUNK
PAIR = 2
BANKS = TILES // PAIR
AHEAD = 6
LAG = 2
SCALAR_ABS_TILES = 1.375
LATE_ABS_TILES = 2

SORTED_TILES = 1

SIGNLESS = 0x7FFF7FFF

FLOPS = 2 * 2 * TOKENS * IN * OUT


def tile_skanlinear_t_kernel(tc, x, weight, out):
    nc = tc.nc
    x_rows = x.flatten_outer_dims()

    with ExitStack() as stack:
        const = stack.enter_context(tc.tile_pool(name="const", bufs=1))
        sorted_pool = stack.enter_context(tc.tile_pool(name="sorted", bufs=LAG + 1))
        x_pool = stack.enter_context(tc.tile_pool(name="x", bufs=AHEAD + 1))
        grouped_pool = stack.enter_context(tc.tile_pool(name="grouped", bufs=3))
        codes_pool = stack.enter_context(tc.tile_pool(name="codes", bufs=LAG + 1))
        y_pool = stack.enter_context(tc.tile_pool(name="y", bufs=(CHUNKS - 1) * BANKS + TILES))
        xt_pool = stack.enter_context(tc.psum_pool(name="xt", bufs=4))
        acc_pool = stack.enter_context(tc.psum_pool(name="acc", bufs=4))
        stack.enter_context(tc.manual_schedule())

        ident_f32 = const.tile([P, P], F32, align_bytes=256)
        make_identity(nc, ident_f32[:])
        ident_bf16 = const.tile([P, P], BF16)
        make_identity(nc, ident_bf16[:])

        def load_chunk(c, pieces):
            x_sb = x_pool.tile([P, TILES * IN], BF16, name="x_sb", align_bytes=256)
            rows = x_rows[c * CHUNK : (c + 1) * CHUNK, :].rearrange("(p j) k -> p (j k)", j=TILES)
            width = TILES * IN // pieces
            for i in range(pieces):
                cols = slice(i * width, (i + 1) * width)
                nc.sync.dma_start(out=x_sb[:, cols], in_=rows[:, cols])
            return x_sb

        x_tiles = [load_chunk(0, TILES)]
        w_rows = []
        for t in range(OUT_TILES):
            w_rows.append(const.tile([P, IN + 2], BF16, name="w_rows%d" % t, align_bytes=256))
            nc.sync.dma_start(out=w_rows[t][:, : IN + 1], in_=weight[t * P : (t + 1) * P, :])
        x_tiles.append(load_chunk(1, TILES))
        x_tiles.append(load_chunk(2, TILES))
        for c in range(3, AHEAD):
            x_tiles.append(load_chunk(c, 1))

        def transpose_rows(row_words, grouped_words, is_sorted=False):
            xt = xt_pool.tile([P, ROW_WORDS], F32, name="xt")
            for b in range(BLOCKS):
                g, u = divmod(b, HALVES)
                if is_sorted:
                    words = slice(b * P, (b + 1) * P)
                else:
                    words = slice(g * P * HALVES + u, (g + 1) * P * HALVES, HALVES)
                nc.tensor.transpose(xt[:, b * P : (b + 1) * P], row_words[:, words], ident_f32[:])
            nc.scalar.copy(
                out=grouped_words,
                in_=xt[:].rearrange("p (g u r) -> p g r u", g=PASSES, u=HALVES),
            )

        def clear_signs(absolute, values):
            nc.vector.tensor_single_scalar(
                out=absolute.bitcast(I32),
                in_=values.bitcast(I32),
                scalar=SIGNLESS,
                op=ALU.bitwise_and,
            )

        def quantise(operand, values):
            codes, scales = operand
            nc.vector.quantize_mx(out=codes[:].bitcast(FP8X4), scales=scales[:], in_=values[:])

        w_signed = [
            const.tile([P, PASSES * OUT], U32, name="w_codes", align_bytes=256),
            const.tile([P, PASSES * OUT], U8, name="w_scales", align_bytes=256),
        ]
        w_absolute = [
            const.tile([P, PASSES * OUT], U32, name="w_abs_codes", align_bytes=256),
            const.tile([P, PASSES * OUT], U8, name="w_abs_scales", align_bytes=256),
        ]
        bias = const.tile([P, PAIR * OUT], F32)

        w_grouped = const.tile([P, PASSES * OUT * PACK], BF16, align_bytes=256)
        w_grouped_abs = const.tile([P, PASSES * OUT * PACK], BF16, align_bytes=256)

        def transpose_weight():
            w_grouped_words = w_grouped[:].bitcast(F32).rearrange(
                "p (g o u) -> p g o u", g=PASSES, u=HALVES
            )
            for t in range(OUT_TILES):
                transpose_rows(
                    w_rows[t][:].bitcast(F32), w_grouped_words[:, :, t * P : (t + 1) * P, :]
                )

        def spread_bias():
            bias_ps = acc_pool.tile([P, PAIR, OUT], F32, name="bias_ps", tag="acc")
            for i in range(PAIR):
                for t in range(OUT_TILES):
                    nc.tensor.matmul(
                        out=bias_ps[:, i, t * P : (t + 1) * P],
                        lhsT=w_rows[t][:, IN : IN + 1].to_broadcast([P, P]),
                        rhs=ident_bf16[:],
                        start=True,
                        stop=True,
                    )
            nc.scalar.activation(
                out=bias[:], in_=bias_ps[:].rearrange("p i o -> p (i o)"), func=ACT.Relu
            )

        def quantise_weight():
            clear_signs(w_grouped_abs[:], w_grouped[:])
            quantise(w_signed, w_grouped)
            quantise(w_absolute, w_grouped_abs)

        def scalar_abs_cols(c):
            if c < LAG:
                return 0
            return int((SCALAR_ABS_TILES if c < CHUNKS - LAG else LATE_ABS_TILES) * IN)

        sorted_of = {}
        grouped_of = {}
        grouped_abs_of = {}
        signed_of = {}
        absolute_of = {}
        acc_of = {}

        def first_sorted(c):
            return TILES if c < 2 * LAG else TILES - SORTED_TILES

        def sort_words(c):
            words = sorted_pool.tile([P, SORTED_TILES * ROW_WORDS], F32, name="sorted_words", align_bytes=256)
            nc.scalar.copy(
                out=words[:].rearrange("p (b u i) -> p b u i", u=HALVES, i=P),
                in_=x_tiles[c][:]
                .bitcast(F32)[:, first_sorted(c) * ROW_WORDS :]
                .rearrange("p (b i u) -> p b u i", u=HALVES, i=P),
            )
            sorted_of[c] = words

        def transpose_chunk(c):
            grouped = grouped_pool.tile([P, TILES * IN], BF16, name="grouped", align_bytes=256)
            grouped_words = grouped[:].bitcast(F32).rearrange(
                "p (j g r u) -> p j g r u", j=TILES, g=PASSES, u=HALVES
            )
            grouped_abs = grouped_pool.tile(
                [P, TILES * IN], BF16, name="grouped_abs", align_bytes=256
            )
            x_words = x_tiles[c][:].bitcast(F32)
            for j in range(TILES):
                if j < first_sorted(c):
                    row_words = x_words[:, j * ROW_WORDS : (j + 1) * ROW_WORDS]
                else:
                    at = (j - first_sorted(c)) * ROW_WORDS
                    row_words = sorted_of[c][:, at : at + ROW_WORDS]
                transpose_rows(row_words, grouped_words[:, j], j >= first_sorted(c))
            if scalar_abs_cols(c):
                cols = slice(0, scalar_abs_cols(c))
                nc.scalar.activation(out=grouped_abs[:, cols], in_=grouped[:, cols], func=ACT.Abs)
            grouped_of[c] = grouped
            grouped_abs_of[c] = grouped_abs

        def new_operand(kind):
            width = TILES * PASSES * P
            return [
                codes_pool.tile([P, width], U32, name=kind + "_codes", align_bytes=256),
                codes_pool.tile([P, width], U8, name=kind + "_scales", align_bytes=256),
            ]

        def clear_signs_of_chunk(c):
            cols = slice(scalar_abs_cols(c), TILES * IN)
            clear_signs(grouped_abs_of[c][:, cols], grouped_of[c][:, cols])

        def quantise_by_blocks(c):
            signed_of[c] = new_operand("signed")
            absolute_of[c] = new_operand("absolute")

            def part(operand, values, j):
                codes, scales = operand
                words = slice(j * PASSES * P, (j + 1) * PASSES * P)
                nc.vector.quantize_mx(
                    out=codes[:, words].bitcast(FP8X4),
                    scales=scales[:, words],
                    in_=values[:, j * IN : (j + 1) * IN],
                )

            for j in range(TILES + 1):
                if j < TILES:
                    cols = slice(j * IN, (j + 1) * IN)
                    clear_signs(grouped_abs_of[c][:, cols], grouped_of[c][:, cols])
                if j > 0:
                    part(absolute_of[c], grouped_abs_of[c], j - 1)
                if j < TILES:
                    part(signed_of[c], grouped_of[c], j)

        def quantise_signed(c):
            signed_of[c] = new_operand("signed")
            quantise(signed_of[c], grouped_of[c])

        def quantise_absolute(c):
            absolute_of[c] = new_operand("absolute")
            halves = 1 if c < CHUNKS - 1 else 2
            codes, scales = absolute_of[c]
            width = TILES * PASSES * P // halves
            for i in range(halves):
                words = slice(i * width, (i + 1) * width)
                nc.vector.quantize_mx(
                    out=codes[:, words].bitcast(FP8X4),
                    scales=scales[:, words],
                    in_=grouped_abs_of[c][:, i * width * PACK : (i + 1) * width * PACK],
                )

        def share(c):
            return PAIR if c < CHUNKS - 1 else 1

        def multiply_chunk(c):
            products = ((signed_of[c], w_signed), (absolute_of[c], w_absolute))

            def multiply_block(j, n):
                x_operand, w_operand = products[n]
                for g in range(PASSES):
                    rows = slice((j * PASSES + g) * P, (j * PASSES + g + 1) * P)
                    cols = slice(g * OUT, (g + 1) * OUT)
                    nc.tensor.matmul_mx(
                        out=acc_of[c][j // share(c)][:, j % share(c), :],
                        lhsT=x_operand[0][:, rows].bitcast(FP8X4),
                        lhsT_scale=x_operand[1][:, rows],
                        rhs=w_operand[0][:, cols].bitcast(FP8X4),
                        rhs_scale=w_operand[1][:, cols],
                        start=(n == 0 and g == 0),
                        stop=(n == 1 and g == PASSES - 1),
                    )

            acc_of[c] = []
            if c < CHUNKS - 1:
                for j in range(TILES):
                    if j % share(c) == 0:
                        acc = acc_pool.tile([P, PAIR, OUT], F32, name="acc")
                        acc_of[c].append(acc)
                    multiply_block(j, 0)
                    multiply_block(j, 1)
            else:
                for j in range(TILES):
                    acc = xt_pool.tile([P, PAIR, OUT], F32, name="last_acc", tag="xt")
                    acc_of[c].append(acc)
                    multiply_block(j, 0)
                for j in range(TILES):
                    multiply_block(j, 1)

        def finish_bank(c, h):
            width = share(c) * OUT
            y = y_pool.tile([P, PAIR * OUT], F32, name="y")
            sums = acc_of[c][h][:].rearrange("p i o -> p (i o)")[:, :width]
            if (c, h) == (CHUNKS - 1, 0):
                nc.scalar.mul(y[:, :width], sums, 0.5)
                nc.gpsimd.tensor_tensor(
                    out=y[:, :width], in0=y[:, :width], in1=bias[:, :width], op=ALU.add
                )
            else:
                nc.vector.scalar_tensor_tensor(
                    out=y[:, :width],
                    in0=sums,
                    scalar=0.5,
                    in1=bias[:, :width],
                    op0=ALU.mult,
                    op1=ALU.add,
                )
            out_chunk = out[c * CHUNK : (c + 1) * CHUNK, :].rearrange("(p j) o -> p (j o)", j=TILES)
            nc.sync.dma_start(out=out_chunk[:, h * width : (h + 1) * width], in_=y[:, :width])

        for s in range(CHUNKS + LAG):
            if s < CHUNKS:
                transpose_chunk(s)
            if LAG <= s < CHUNKS - LAG:
                sort_words(s + LAG)
            if s == 0:
                transpose_weight()
            if s == 1:
                spread_bias()
            if s >= LAG:
                multiply_chunk(s - LAG)
            if s == 0:
                quantise_by_blocks(s)
                quantise_weight()
            elif s < CHUNKS:
                clear_signs_of_chunk(s)
                quantise_signed(s)
            finished = TILES // share(s - LAG) if s >= LAG else 0
            before = min(finished, 1) if s < CHUNKS - 1 else finished
            for h in range(before):
                finish_bank(s - LAG, h)
            if 0 < s < CHUNKS:
                quantise_absolute(s)
            for h in range(before, finished):
                finish_bank(s - LAG, h)
            if s + AHEAD < CHUNKS:
                x_tiles.append(load_chunk(s + AHEAD, 1))
